import numpy as np
import ml_dtypes


def mxq(x, axis, fmt="e4m3"):
    dtype, down = {"e4m3": (ml_dtypes.float8_e4m3fn, 7), "e5m2": (ml_dtypes.float8_e5m2, 14)}[fmt]
    v = np.moveaxis(np.asarray(x, np.float32).astype(ml_dtypes.bfloat16).astype(np.float64), axis, -1)
    blocks = v.reshape(v.shape[:-1] + (-1, 32))
    amax = np.abs(blocks).max(-1, keepdims=True)
    byte = np.maximum(np.where(amax > 0, np.frexp(amax)[1] - 1 + 127, 0) - down, 1)
    scale = np.exp2(byte - 127.0)
    codes = (blocks / scale).astype(np.float32).astype(dtype).astype(np.float64)
    return np.moveaxis((codes * scale).reshape(v.shape), -1, axis)


WIDE = False


def mx_kscale(k):
    if not WIDE:
        return np.ones(k)
    levels = np.array([20, -20, 10, -10, 0])
    a = np.random.permutation(np.resize(levels, k // 512 * 4)).reshape(k // 512, 4)
    idx = np.arange(k)
    return np.exp2(a[idx // 512, idx % 128 // 32])


BF16 = ml_dtypes.bfloat16


def bf(x):
    return np.asarray(x, np.float32).astype(BF16)


def f64(x):
    return np.asarray(x).astype(np.float64)


B, CIN, H, W, COUT, N = 2, 1024, 32, 32, 512, 9


def setup_inputs():
    u = mx_kscale(COUT)
    x = np.random.standard_normal((B, CIN, H, W))
    weights = np.random.standard_normal((N, COUT, CIN, 1, 1)) * np.sqrt(N) / np.sqrt(CIN) / u[None, :, None, None, None]
    biases = np.random.standard_normal((N, COUT)) * 0.5 * np.sqrt(N)
    g = np.random.standard_normal((B, COUT, H, W)) * np.exp2(np.random.randint(-12, 1, (B, 1, H, W))) * 16.0 * u[None, :, None, None]
    return {"x": bf(x), "weights": bf(weights), "biases": bf(biases), "grad_out": bf(g)}


def reference(x, weights, biases, grad_out):
    w = np.mean(f64(weights), axis=0)[:, :, 0, 0]
    gx = np.einsum('bohw,oc->bchw', mxq(f64(grad_out), 1, "e5m2"), mxq(w, 0, "e4m3"), optimize=True)
    return gx

@@ -1,0 +1,180 @@
+from contextlib import ExitStack
+
+import concourse.mybir as mybir
+from concourse.masks import make_identity
+
+F32 = mybir.dt.float32
+BF16 = mybir.dt.bfloat16
+U32 = mybir.dt.uint32
+U8 = mybir.dt.uint8
+E4M3X4 = mybir.dt.float8_e4m3fn_x4
+E5M2X4 = mybir.dt.float8_e5m2_x4
+ADD = mybir.AluOpType.add
+MULT = mybir.AluOpType.mult
+COPY = mybir.ActivationFunctionType.Copy
+
+P = 128
+PACK = 4
+LAYERS = 9
+COUT = 512
+CIN = 1024
+BATCH = 2
+PIX = 1024
+N_TILE = 512
+UNITS = CIN // P
+INV = 1.0 / LAYERS
+
+FLOPS = 2 * BATCH * PIX * COUT * CIN
+BYTES = LAYERS * COUT * CIN * 2 + BATCH * COUT * PIX * 2 + BATCH * CIN * PIX * 4
+
+LOAD_ORDER = ("w0", "w1", "w2", "w3", "g0", "w4", "g1", "w5", "w6", "w7", "w8")
+PE_ORDER = (0, 1, 2, 3, 4, 5, 6, 7, 8)
+PE_PART = (0, 1, 2)
+GROUPS = ((1, 2), (3, 4), (5, 6), (7,))
+VECTOR_EVAC = {7: (1, 3)}
+
+
+def tile_conv_1x1_9_layer_t_kernel(tc, x, weights, biases, grad_out, out):
+    nc = tc.nc
+    w_dram = weights.rearrange("i (p t) c a b -> i p t (c a b)", t=PACK)
+    g_dram = grad_out.rearrange("b (p t) h v -> b p t (h v)", t=PACK)
+    o_dram = out.rearrange("b (u m) h v -> b u m (h v)", m=P)
+
+    with ExitStack() as ctx:
+        keep = ctx.enter_context(tc.tile_pool(name="keep", bufs=1))
+        stage = ctx.enter_context(tc.tile_pool(name="stage", bufs=8))
+        psum = ctx.enter_context(tc.psum_pool(name="psum", bufs=8))
+        ctx.enter_context(tc.manual_schedule())
+
+        ident = keep.tile([P, P], BF16, name="ident")
+        make_identity(nc, ident[:])
+
+        w_raw = [keep.tile([P, PACK, CIN], BF16, name="w_raw%d" % i) for i in range(LAYERS)]
+        g_raw = [keep.tile([P, PACK, PIX], BF16, name="g_raw%d" % b) for b in range(BATCH)]
+        for item in LOAD_ORDER:
+            k = int(item[1])
+            if item[0] == "w":
+                nc.sync.dma_start(out=w_raw[k][:], in_=w_dram[k])
+            else:
+                nc.sync.dma_start(out=g_raw[k][:], in_=g_dram[k])
+
+        g_grp = [keep.tile([P, PIX, PACK], BF16, name="g_grp%d" % b, align_bytes=64) for b in range(BATCH)]
+        g_codes = keep.tile([P, BATCH * PIX], U32, name="g_codes", align_bytes=64)
+        g_scales = keep.tile([P, BATCH * PIX], U8, name="g_scales", align_bytes=64)
+        w_grp = keep.tile([P, CIN, PACK], BF16, name="w_grp", align_bytes=64)
+        w_codes = keep.tile([P, CIN], U32, name="w_codes", align_bytes=64)
+        w_scales = keep.tile([P, CIN], U8, name="w_scales", align_bytes=64)
+        acc = [None] + [keep.tile([P, PACK, P], F32, name="acc%d" % u) for u in range(1, UNITS)]
+
+        def cols(u):
+            return slice(u * P, (u + 1) * P)
+
+        sum_all = psum.tile([P, N_TILE], F32, name="bank")
+        sum_part = psum.tile([P, N_TILE], F32, name="bank")
+        for i in PE_ORDER:
+            nc.tensor.matmul(
+                out=sum_all[:].rearrange("p (t c) -> p t c", t=PACK),
+                lhsT=ident[:],
+                rhs=w_raw[i][:, :, cols(0)],
+                start=(i == PE_ORDER[0]),
+                stop=(i == PE_ORDER[-1]),
+            )
+            if i in PE_PART:
+                nc.tensor.matmul(
+                    out=sum_part[:].rearrange("p (t c) -> p t c", t=PACK),
+                    lhsT=ident[:],
+                    rhs=w_raw[i][:, :, cols(1)],
+                    start=(i == PE_PART[0]),
+                    stop=(i == PE_PART[-1]),
+                )
+
+        for n in range(4):
+            b, h = divmod(n, 2)
+            span = slice(h * N_TILE, (h + 1) * N_TILE)
+            nc.scalar.copy(
+                out=g_grp[b][:, span, :].rearrange("p (c i) t -> p c t i", i=4),
+                in_=g_raw[b][:, :, span].rearrange("p t (c i) -> p c t i", i=4),
+            )
+        nc.scalar.activation(
+            out=w_grp[:, cols(0), :],
+            in_=sum_all[:].rearrange("p (t c) -> p c t", t=PACK),
+            func=COPY,
+            scale=INV,
+        )
+
+        def add_layer(u, i):
+            nc.vector.tensor_tensor(out=acc[u][:], in0=acc[u][:], in1=w_raw[i][:, :, cols(u)], op=ADD)
+
+        def quantise_g(n):
+            b, h = divmod(n, 2)
+            span = slice(h * N_TILE, (h + 1) * N_TILE)
+            nc.vector.quantize_mx(
+                out=g_codes[:, n * N_TILE : (n + 1) * N_TILE].bitcast(E5M2X4),
+                scales=g_scales[:, n * N_TILE : (n + 1) * N_TILE],
+                in_=g_grp[b][:, span, :].rearrange("p n t -> p (n t)"),
+            )
+
+        def finish_mean(u):
+            nc.vector.tensor_scalar(
+                out=w_grp[:, cols(u), :],
+                in0=acc[u][:].rearrange("p t c -> p c t"),
+                scalar1=INV,
+                scalar2=None,
+                op0=MULT,
+            )
+
+        def produce(u):
+            nc.vector.quantize_mx(
+                out=w_codes[:, cols(u)].bitcast(E4M3X4),
+                scales=w_scales[:, cols(u)],
+                in_=w_grp[:, cols(u), :].rearrange("p c t -> p (c t)"),
+            )
+            for b in range(BATCH):
+                stg = stage.tile([P, PIX], F32, name="stg")
+                for h in range(2):
+                    n = 2 * b + h
+                    bank = psum.tile([P, N_TILE], F32, name="bank")
+                    nc.tensor.matmul_mx(
+                        out=bank[:],
+                        lhsT=w_codes[:, cols(u)].bitcast(E4M3X4),
+                        lhsT_scale=w_scales[:, cols(u)],
+                        rhs=g_codes[:, n * N_TILE : (n + 1) * N_TILE].bitcast(E5M2X4),
+                        rhs_scale=g_scales[:, n * N_TILE : (n + 1) * N_TILE],
+                        start=True,
+                        stop=True,
+                    )
+                    half = stg[:, h * N_TILE : (h + 1) * N_TILE]
+                    if n in VECTOR_EVAC.get(u, ()):
+                        nc.vector.tensor_copy(out=half, in_=bank[:])
+                    else:
+                        nc.scalar.copy(out=half, in_=bank[:])
+                nc.sync.dma_start(out=o_dram[b, u], in_=stg[:])
+
+        rest = range(2, UNITS)
+        for u in rest:
+            nc.vector.tensor_tensor(out=acc[u][:], in0=w_raw[0][:, :, cols(u)], in1=w_raw[1][:, :, cols(u)], op=ADD)
+        for u in rest:
+            add_layer(u, 2)
+        nc.vector.tensor_tensor(
+            out=acc[1][:],
+            in0=sum_part[:].rearrange("p (t c) -> p t c", t=PACK),
+            in1=w_raw[3][:, :, cols(1)],
+            op=ADD,
+        )
+        for u in rest:
+            add_layer(u, 3)
+        quantise_g(0)
+        for u in range(1, UNITS):
+            add_layer(u, 4)
+        for gi, group in enumerate(GROUPS):
+            for i in range(5, LAYERS):
+                if gi == 0 and i < 8:
+                    quantise_g(i - 4)
+                for u in group:
+                    add_layer(u, i)
+            if gi == 0:
+                produce(0)
+            for u in group:
+                finish_mean(u)
+            for u in group:
+                produce(u)

@@ -27,10 +27,13 @@ INV = 1.0 / LAYERS
 FLOPS = 2 * BATCH * PIX * COUT * CIN
 BYTES = LAYERS * COUT * CIN * 2 + BATCH * COUT * PIX * 2 + BATCH * CIN * PIX * 4
 
-LOAD_ORDER = ("w0", "w1", "w2", "w3", "g0", "w4", "g1", "w5", "w6", "w7", "w8")
-PE_ORDER = (0, 1, 2, 3, 4, 5, 6, 7, 8)
-PE_PART = (0, 1, 2)
-GROUPS = ((1, 2), (3, 4), (5, 6), (7,))
+SPLIT_T = (0, 1)
+SPLIT_C = (7, 8)
+STRIP_UNITS = 2
+STRIP = STRIP_UNITS * P
+LOAD_ORDER = ("w0a", "w1a", "w0b", "w1b", "w2", "w3", "g0", "w4", "g1", "w5", "w6", "w7e", "w8e", "w7f", "w8f")
+PE_ORDER = (2, 0, 1, 3, 4, 5, 6, 7, 8)
+PE_PART = (2, 0, 3)
 VECTOR_EVAC = {7: (1, 3)}
 
 
@@ -44,19 +47,36 @@ def tile_conv_1x1_9_layer_t_kernel(tc, x, weights, biases, grad_out, out):
         keep = ctx.enter_context(tc.tile_pool(name="keep", bufs=1))
         stage = ctx.enter_context(tc.tile_pool(name="stage", bufs=8))
         psum = ctx.enter_context(tc.psum_pool(name="psum", bufs=8))
-        ctx.enter_context(tc.manual_schedule())
 
         ident = keep.tile([P, P], BF16, name="ident")
         make_identity(nc, ident[:])
 
-        w_raw = [keep.tile([P, PACK, CIN], BF16, name="w_raw%d" % i) for i in range(LAYERS)]
+        w_tiles = {}
+        for i in range(LAYERS):
+            if i in SPLIT_T:
+                for h in range(2):
+                    w_tiles[(i, "ab"[h])] = keep.tile([P, 2, CIN], BF16, name="w%d%s" % (i, "ab"[h]))
+            elif i in SPLIT_C:
+                w_tiles[(i, "e")] = keep.tile([P, PACK, STRIP], BF16, name="w%de" % i)
+                w_tiles[(i, "f")] = keep.tile([P, PACK, CIN - STRIP], BF16, name="w%df" % i)
+            else:
+                w_tiles[(i, "")] = keep.tile([P, PACK, CIN], BF16, name="w%d" % i)
         g_raw = [keep.tile([P, PACK, PIX], BF16, name="g_raw%d" % b) for b in range(BATCH)]
         for item in LOAD_ORDER:
             k = int(item[1])
-            if item[0] == "w":
-                nc.sync.dma_start(out=w_raw[k][:], in_=w_dram[k])
-            else:
+            part = item[2:]
+            if item[0] == "g":
                 nc.sync.dma_start(out=g_raw[k][:], in_=g_dram[k])
+            elif part == "a":
+                nc.sync.dma_start(out=w_tiles[(k, part)][:], in_=w_dram[k][:, 0:2, :])
+            elif part == "b":
+                nc.sync.dma_start(out=w_tiles[(k, part)][:], in_=w_dram[k][:, 2:4, :])
+            elif part == "e":
+                nc.sync.dma_start(out=w_tiles[(k, part)][:], in_=w_dram[k][:, :, 0:STRIP])
+            elif part == "f":
+                nc.sync.dma_start(out=w_tiles[(k, part)][:], in_=w_dram[k][:, :, STRIP:CIN])
+            else:
+                nc.sync.dma_start(out=w_tiles[(k, part)][:], in_=w_dram[k])
 
         g_grp = [keep.tile([P, PIX, PACK], BF16, name="g_grp%d" % b, align_bytes=64) for b in range(BATCH)]
         g_codes = keep.tile([P, BATCH * PIX], U32, name="g_codes", align_bytes=64)
@@ -69,24 +89,34 @@ def tile_conv_1x1_9_layer_t_kernel(tc, x, weights, biases, grad_out, out):
         def cols(u):
             return slice(u * P, (u + 1) * P)
 
+        def layer(i, u):
+            if i in SPLIT_C:
+                if u < STRIP_UNITS:
+                    return w_tiles[(i, "e")][:, :, cols(u)]
+                return w_tiles[(i, "f")][:, :, cols(u - STRIP_UNITS)]
+            return w_tiles[(i, "")][:, :, cols(u)]
+
+        def half_layer(i, h, u):
+            return w_tiles[(i, "ab"[h])][:, :, cols(u)]
+
+        def rows(tile_ap, h):
+            return tile_ap.rearrange("p (t c) -> p t c", t=PACK)[:, 2 * h : 2 * h + 2, :]
+
         sum_all = psum.tile([P, N_TILE], F32, name="bank")
         sum_part = psum.tile([P, N_TILE], F32, name="bank")
-        for i in PE_ORDER:
-            nc.tensor.matmul(
-                out=sum_all[:].rearrange("p (t c) -> p t c", t=PACK),
-                lhsT=ident[:],
-                rhs=w_raw[i][:, :, cols(0)],
-                start=(i == PE_ORDER[0]),
-                stop=(i == PE_ORDER[-1]),
-            )
-            if i in PE_PART:
-                nc.tensor.matmul(
-                    out=sum_part[:].rearrange("p (t c) -> p t c", t=PACK),
-                    lhsT=ident[:],
-                    rhs=w_raw[i][:, :, cols(1)],
-                    start=(i == PE_PART[0]),
-                    stop=(i == PE_PART[-1]),
-                )
+        for target, unit, order in ((sum_part, 1, PE_PART), (sum_all, 0, PE_ORDER)):
+            for i in order:
+                if i in SPLIT_T:
+                    for h in range(2):
+                        nc.tensor.matmul(out=rows(target[:], h), lhsT=ident[:], rhs=half_layer(i, h, unit), start=False, stop=False)
+                else:
+                    nc.tensor.matmul(
+                        out=target[:].rearrange("p (t c) -> p t c", t=PACK),
+                        lhsT=ident[:],
+                        rhs=layer(i, unit),
+                        start=(i == order[0]),
+                        stop=(i == order[-1]),
+                    )
 
         for n in range(4):
             b, h = divmod(n, 2)
@@ -102,8 +132,15 @@ def tile_conv_1x1_9_layer_t_kernel(tc, x, weights, biases, grad_out, out):
             scale=INV,
         )
 
+        def first_add(u, h):
+            span = acc[u][:, 2 * h : 2 * h + 2, :]
+            if u == 1:
+                nc.vector.tensor_tensor(out=span, in0=rows(sum_part[:], h), in1=half_layer(1, h, u), op=ADD)
+            else:
+                nc.vector.tensor_tensor(out=span, in0=half_layer(0, h, u), in1=half_layer(1, h, u), op=ADD)
+
         def add_layer(u, i):
-            nc.vector.tensor_tensor(out=acc[u][:], in0=acc[u][:], in1=w_raw[i][:, :, cols(u)], op=ADD)
+            nc.vector.tensor_tensor(out=acc[u][:], in0=acc[u][:], in1=layer(i, u), op=ADD)
 
         def quantise_g(n):
             b, h = divmod(n, 2)
@@ -150,31 +187,15 @@ def tile_conv_1x1_9_layer_t_kernel(tc, x, weights, biases, grad_out, out):
                         nc.scalar.copy(out=half, in_=bank[:])
                 nc.sync.dma_start(out=o_dram[b, u], in_=stg[:])
 
-        rest = range(2, UNITS)
-        for u in rest:
-            nc.vector.tensor_tensor(out=acc[u][:], in0=w_raw[0][:, :, cols(u)], in1=w_raw[1][:, :, cols(u)], op=ADD)
-        for u in rest:
-            add_layer(u, 2)
-        nc.vector.tensor_tensor(
-            out=acc[1][:],
-            in0=sum_part[:].rearrange("p (t c) -> p t c", t=PACK),
-            in1=w_raw[3][:, :, cols(1)],
-            op=ADD,
-        )
-        for u in rest:
-            add_layer(u, 3)
-        quantise_g(0)
+        for n in range(4):
+            quantise_g(n)
+        produce(0)
         for u in range(1, UNITS):
-            add_layer(u, 4)
-        for gi, group in enumerate(GROUPS):
-            for i in range(5, LAYERS):
-                if gi == 0 and i < 8:
-                    quantise_g(i - 4)
-                for u in group:
-                    add_layer(u, i)
-            if gi == 0:
-                produce(0)
-            for u in group:
-                finish_mean(u)
-            for u in group:
-                produce(u)
+            first_add(u, 0)
+            first_add(u, 1)
+            for i in range(2, LAYERS):
+                if u == 1 and i in PE_PART:
+                    continue
+                add_layer(u, i)
+            finish_mean(u)
+            produce(u)

@@ -27,14 +27,15 @@ INV = 1.0 / LAYERS
 FLOPS = 2 * BATCH * PIX * COUT * CIN
 BYTES = LAYERS * COUT * CIN * 2 + BATCH * COUT * PIX * 2 + BATCH * CIN * PIX * 4
 
-SPLIT_T = (0, 1)
-SPLIT_C = (7, 8)
+SPLIT_C = (6, 7, 8)
 STRIP_UNITS = 2
 STRIP = STRIP_UNITS * P
-LOAD_ORDER = ("w0a", "w1a", "w0b", "w1b", "w2", "w3", "g0", "w4", "g1", "w5", "w6", "w7e", "w8e", "w7f", "w8f")
-PE_ORDER = (2, 0, 1, 3, 4, 5, 6, 7, 8)
-PE_PART = (2, 0, 3)
-VECTOR_EVAC = {7: (1, 3)}
+WIDE = UNITS - STRIP_UNITS
+ROW_PIECES = ((0, 1), (1, 2), (2, 4))
+BASE_LAYERS = (2, 3, 4)
+BASE_PIECES = {2: ((0, 2), (2, 4)), 3: ((0, 4),), 4: ((0, 4),)}
+PE_PART = (0, 1, 2)
+LAST = UNITS - 1
 
 
 def tile_conv_1x1_9_layer_t_kernel(tc, x, weights, biases, grad_out, out):
@@ -51,32 +52,29 @@ def tile_conv_1x1_9_layer_t_kernel(tc, x, weights, biases, grad_out, out):
         ident = keep.tile([P, P], BF16, name="ident")
         make_identity(nc, ident[:])
 
-        w_tiles = {}
-        for i in range(LAYERS):
-            if i in SPLIT_T:
-                for h in range(2):
-                    w_tiles[(i, "ab"[h])] = keep.tile([P, 2, CIN], BF16, name="w%d%s" % (i, "ab"[h]))
-            elif i in SPLIT_C:
-                w_tiles[(i, "e")] = keep.tile([P, PACK, STRIP], BF16, name="w%de" % i)
-                w_tiles[(i, "f")] = keep.tile([P, PACK, CIN - STRIP], BF16, name="w%df" % i)
-            else:
-                w_tiles[(i, "")] = keep.tile([P, PACK, CIN], BF16, name="w%d" % i)
+        w_full = [keep.tile([P, PACK, CIN], BF16, name="w%d" % i) for i in range(SPLIT_C[0])]
+        w_strip = {}
+        w_rest = {}
+        for i in SPLIT_C:
+            w_strip[i] = keep.tile([P, PACK, STRIP], BF16, name="w%de" % i)
+            w_rest[i] = keep.tile([P, PACK, CIN - STRIP], BF16, name="w%df" % i)
         g_raw = [keep.tile([P, PACK, PIX], BF16, name="g_raw%d" % b) for b in range(BATCH)]
-        for item in LOAD_ORDER:
-            k = int(item[1])
-            part = item[2:]
-            if item[0] == "g":
-                nc.sync.dma_start(out=g_raw[k][:], in_=g_dram[k])
-            elif part == "a":
-                nc.sync.dma_start(out=w_tiles[(k, part)][:], in_=w_dram[k][:, 0:2, :])
-            elif part == "b":
-                nc.sync.dma_start(out=w_tiles[(k, part)][:], in_=w_dram[k][:, 2:4, :])
-            elif part == "e":
-                nc.sync.dma_start(out=w_tiles[(k, part)][:], in_=w_dram[k][:, :, 0:STRIP])
-            elif part == "f":
-                nc.sync.dma_start(out=w_tiles[(k, part)][:], in_=w_dram[k][:, :, STRIP:CIN])
-            else:
-                nc.sync.dma_start(out=w_tiles[(k, part)][:], in_=w_dram[k])
+
+        for r0, r1 in ROW_PIECES:
+            for i in (0, 1):
+                nc.sync.dma_start(out=w_full[i][:, r0:r1, :], in_=w_dram[i][:, r0:r1, :])
+        for i in (2, 3):
+            for r0, r1 in BASE_PIECES[i]:
+                nc.sync.dma_start(out=w_full[i][:, r0:r1, :], in_=w_dram[i][:, r0:r1, :])
+        nc.sync.dma_start(out=g_raw[0][:], in_=g_dram[0])
+        nc.sync.dma_start(out=w_full[4][:], in_=w_dram[4])
+        nc.sync.dma_start(out=g_raw[1][:], in_=g_dram[1])
+        for i in range(5, SPLIT_C[0]):
+            nc.sync.dma_start(out=w_full[i][:], in_=w_dram[i])
+        for i in SPLIT_C:
+            nc.sync.dma_start(out=w_strip[i][:], in_=w_dram[i][:, :, 0:STRIP])
+        for i in SPLIT_C:
+            nc.sync.dma_start(out=w_rest[i][:], in_=w_dram[i][:, :, STRIP:CIN])
 
         g_grp = [keep.tile([P, PIX, PACK], BF16, name="g_grp%d" % b, align_bytes=64) for b in range(BATCH)]
         g_codes = keep.tile([P, BATCH * PIX], U32, name="g_codes", align_bytes=64)
@@ -84,7 +82,8 @@ def tile_conv_1x1_9_layer_t_kernel(tc, x, weights, biases, grad_out, out):
         w_grp = keep.tile([P, CIN, PACK], BF16, name="w_grp", align_bytes=64)
         w_codes = keep.tile([P, CIN], U32, name="w_codes", align_bytes=64)
         w_scales = keep.tile([P, CIN], U8, name="w_scales", align_bytes=64)
-        acc = [None] + [keep.tile([P, PACK, P], F32, name="acc%d" % u) for u in range(1, UNITS)]
+        acc_one = keep.tile([P, PACK, P], F32, name="acc_one")
+        acc_wide = keep.tile([P, WIDE, PACK, P], F32, name="acc_wide")
 
         def cols(u):
             return slice(u * P, (u + 1) * P)
@@ -92,31 +91,29 @@ def tile_conv_1x1_9_layer_t_kernel(tc, x, weights, biases, grad_out, out):
         def layer(i, u):
             if i in SPLIT_C:
                 if u < STRIP_UNITS:
-                    return w_tiles[(i, "e")][:, :, cols(u)]
-                return w_tiles[(i, "f")][:, :, cols(u - STRIP_UNITS)]
-            return w_tiles[(i, "")][:, :, cols(u)]
+                    return w_strip[i][:, :, cols(u)]
+                return w_rest[i][:, :, cols(u - STRIP_UNITS)]
+            return w_full[i][:, :, cols(u)]
 
-        def half_layer(i, h, u):
-            return w_tiles[(i, "ab"[h])][:, :, cols(u)]
+        def wide(i, r0, r1):
+            return w_full[i][:, r0:r1, STRIP:CIN].rearrange("p t (u c) -> p u t c", u=WIDE)
 
-        def rows(tile_ap, h):
-            return tile_ap.rearrange("p (t c) -> p t c", t=PACK)[:, 2 * h : 2 * h + 2, :]
+        def acc(u):
+            if u == 1:
+                return acc_one[:]
+            return acc_wide[:, u - STRIP_UNITS, :, :]
 
-        sum_all = psum.tile([P, N_TILE], F32, name="bank")
         sum_part = psum.tile([P, N_TILE], F32, name="bank")
-        for target, unit, order in ((sum_part, 1, PE_PART), (sum_all, 0, PE_ORDER)):
+        sum_all = psum.tile([P, N_TILE], F32, name="bank")
+        for target, unit, order in ((sum_part, 1, PE_PART), (sum_all, 0, tuple(range(LAYERS)))):
             for i in order:
-                if i in SPLIT_T:
-                    for h in range(2):
-                        nc.tensor.matmul(out=rows(target[:], h), lhsT=ident[:], rhs=half_layer(i, h, unit), start=False, stop=False)
-                else:
-                    nc.tensor.matmul(
-                        out=target[:].rearrange("p (t c) -> p t c", t=PACK),
-                        lhsT=ident[:],
-                        rhs=layer(i, unit),
-                        start=(i == order[0]),
-                        stop=(i == order[-1]),
-                    )
+                nc.tensor.matmul(
+                    out=target[:].rearrange("p (t c) -> p t c", t=PACK),
+                    lhsT=ident[:],
+                    rhs=layer(i, unit),
+                    start=(i == order[0]),
+                    stop=(i == order[-1]),
+                )
 
         for n in range(4):
             b, h = divmod(n, 2)
@@ -132,15 +129,8 @@ def tile_conv_1x1_9_layer_t_kernel(tc, x, weights, biases, grad_out, out):
             scale=INV,
         )
 
-        def first_add(u, h):
-            span = acc[u][:, 2 * h : 2 * h + 2, :]
-            if u == 1:
-                nc.vector.tensor_tensor(out=span, in0=rows(sum_part[:], h), in1=half_layer(1, h, u), op=ADD)
-            else:
-                nc.vector.tensor_tensor(out=span, in0=half_layer(0, h, u), in1=half_layer(1, h, u), op=ADD)
-
         def add_layer(u, i):
-            nc.vector.tensor_tensor(out=acc[u][:], in0=acc[u][:], in1=layer(i, u), op=ADD)
+            nc.vector.tensor_tensor(out=acc(u), in0=acc(u), in1=layer(i, u), op=ADD)
 
         def quantise_g(n):
             b, h = divmod(n, 2)
@@ -151,23 +141,19 @@ def tile_conv_1x1_9_layer_t_kernel(tc, x, weights, biases, grad_out, out):
                 in_=g_grp[b][:, span, :].rearrange("p n t -> p (n t)"),
             )
 
-        def finish_mean(u):
-            nc.vector.tensor_scalar(
-                out=w_grp[:, cols(u), :],
-                in0=acc[u][:].rearrange("p t c -> p c t"),
-                scalar1=INV,
-                scalar2=None,
-                op0=MULT,
+        def quantise_w(u0, u1):
+            span = slice(u0 * P, u1 * P)
+            nc.vector.quantize_mx(
+                out=w_codes[:, span].bitcast(E4M3X4),
+                scales=w_scales[:, span],
+                in_=w_grp[:, span, :].rearrange("p c t -> p (c t)"),
             )
 
-        def produce(u):
-            nc.vector.quantize_mx(
-                out=w_codes[:, cols(u)].bitcast(E4M3X4),
-                scales=w_scales[:, cols(u)],
-                in_=w_grp[:, cols(u), :].rearrange("p c t -> p (c t)"),
-            )
+        def multiply(u):
+            fine = u in (0, LAST)
             for b in range(BATCH):
-                stg = stage.tile([P, PIX], F32, name="stg")
+                if not fine:
+                    stg = stage.tile([P, PIX], F32, name="stg")
                 for h in range(2):
                     n = 2 * b + h
                     bank = psum.tile([P, N_TILE], F32, name="bank")
@@ -180,22 +166,63 @@ def tile_conv_1x1_9_layer_t_kernel(tc, x, weights, biases, grad_out, out):
                         start=True,
                         stop=True,
                     )
-                    half = stg[:, h * N_TILE : (h + 1) * N_TILE]
-                    if n in VECTOR_EVAC.get(u, ()):
-                        nc.vector.tensor_copy(out=half, in_=bank[:])
+                    if fine:
+                        part = stage.tile([P, N_TILE], F32, name="part")
+                        target = part[:]
                     else:
-                        nc.scalar.copy(out=half, in_=bank[:])
-                nc.sync.dma_start(out=o_dram[b, u], in_=stg[:])
+                        target = stg[:, h * N_TILE : (h + 1) * N_TILE]
+                    if u == LAST and h == 1:
+                        nc.vector.tensor_copy(out=target, in_=bank[:])
+                    else:
+                        nc.scalar.copy(out=target, in_=bank[:])
+                    if fine:
+                        nc.sync.dma_start(out=o_dram[b, u][:, h * N_TILE : (h + 1) * N_TILE], in_=target)
+                if not fine:
+                    nc.sync.dma_start(out=o_dram[b, u], in_=stg[:])
 
+        for r0, r1 in ROW_PIECES:
+            nc.vector.tensor_tensor(out=acc_wide[:, :, r0:r1, :], in0=wide(0, r0, r1), in1=wide(1, r0, r1), op=ADD)
+        for i in BASE_LAYERS:
+            if i == 3:
+                nc.vector.tensor_tensor(
+                    out=acc_one[:],
+                    in0=sum_part[:].rearrange("p (t c) -> p t c", t=PACK),
+                    in1=layer(3, 1),
+                    op=ADD,
+                )
+            if i == 4:
+                add_layer(1, 4)
+            for r0, r1 in BASE_PIECES[i]:
+                nc.vector.tensor_tensor(out=acc_wide[:, :, r0:r1, :], in0=acc_wide[:, :, r0:r1, :], in1=wide(i, r0, r1), op=ADD)
         for n in range(4):
             quantise_g(n)
-        produce(0)
-        for u in range(1, UNITS):
-            first_add(u, 0)
-            first_add(u, 1)
-            for i in range(2, LAYERS):
-                if u == 1 and i in PE_PART:
-                    continue
-                add_layer(u, i)
-            finish_mean(u)
-            produce(u)
+        quantise_w(0, 1)
+        multiply(0)
+        for i in range(5, LAYERS):
+            add_layer(1, i)
+        nc.scalar.activation(
+            out=w_grp[:, cols(1), :],
+            in_=acc_one[:].rearrange("p t c -> p c t"),
+            func=COPY,
+            scale=INV,
+        )
+        quantise_w(1, 2)
+        multiply(1)
+        for u in range(STRIP_UNITS, UNITS):
+            for i in range(5, LAYERS):
+                if u == LAST:
+                    for r0 in (0, 2):
+                        nc.vector.tensor_tensor(
+                            out=acc(u)[:, r0 : r0 + 2, :], in0=acc(u)[:, r0 : r0 + 2, :], in1=layer(i, u)[:, r0 : r0 + 2, :], op=ADD
+                        )
+                else:
+                    add_layer(u, i)
+            nc.vector.tensor_scalar(
+                out=w_grp[:, cols(u), :],
+                in0=acc(u).rearrange("p t c -> p c t"),
+                scalar1=INV,
+                scalar2=None,
+                op0=MULT,
+            )
+            quantise_w(u, u + 1)
+            multiply(u)

@@ -27,13 +27,13 @@ INV = 1.0 / LAYERS
 FLOPS = 2 * BATCH * PIX * COUT * CIN
 BYTES = LAYERS * COUT * CIN * 2 + BATCH * COUT * PIX * 2 + BATCH * CIN * PIX * 4
 
-SPLIT_C = (6, 7, 8)
+SPLIT_C = (7, 8)
 STRIP_UNITS = 2
 STRIP = STRIP_UNITS * P
 WIDE = UNITS - STRIP_UNITS
-ROW_PIECES = ((0, 1), (1, 2), (2, 4))
+ROW_PIECES = ((0, 2), (2, 4))
 BASE_LAYERS = (2, 3, 4)
-BASE_PIECES = {2: ((0, 2), (2, 4)), 3: ((0, 4),), 4: ((0, 4),)}
+BASE_PIECES = {2: ((0, 4),), 3: ((0, 4),), 4: ((0, 4),)}
 PE_PART = (0, 1, 2)
 LAST = UNITS - 1
 
@@ -150,7 +150,7 @@ def tile_conv_1x1_9_layer_t_kernel(tc, x, weights, biases, grad_out, out):
             )
 
         def multiply(u):
-            fine = u in (0, LAST)
+            fine = u in (LAST,)
             for b in range(BATCH):
                 if not fine:
                     stg = stage.tile([P, PIX], F32, name="stg")

@@ -27,14 +27,15 @@ INV = 1.0 / LAYERS
 FLOPS = 2 * BATCH * PIX * COUT * CIN
 BYTES = LAYERS * COUT * CIN * 2 + BATCH * COUT * PIX * 2 + BATCH * CIN * PIX * 4
 
-SPLIT_C = (7, 8)
+SPLIT_C = (6, 7, 8)
 STRIP_UNITS = 2
 STRIP = STRIP_UNITS * P
-WIDE = UNITS - STRIP_UNITS
-ROW_PIECES = ((0, 2), (2, 4))
+WIDE0 = 1
+WIDE = UNITS - WIDE0
+ROW_PIECES = ((0, 1), (1, 2), (2, 3), (3, 4))
 BASE_LAYERS = (2, 3, 4)
-BASE_PIECES = {2: ((0, 4),), 3: ((0, 4),), 4: ((0, 4),)}
-PE_PART = (0, 1, 2)
+BASE_PIECES = {2: ((0, 2), (2, 4)), 3: ((0, 4),), 4: ((0, 4),)}
+PE_PART = (6, 7, 8)
 LAST = UNITS - 1
 
 
@@ -82,7 +83,6 @@ def tile_conv_1x1_9_layer_t_kernel(tc, x, weights, biases, grad_out, out):
         w_grp = keep.tile([P, CIN, PACK], BF16, name="w_grp", align_bytes=64)
         w_codes = keep.tile([P, CIN], U32, name="w_codes", align_bytes=64)
         w_scales = keep.tile([P, CIN], U8, name="w_scales", align_bytes=64)
-        acc_one = keep.tile([P, PACK, P], F32, name="acc_one")
         acc_wide = keep.tile([P, WIDE, PACK, P], F32, name="acc_wide")
 
         def cols(u):
@@ -96,17 +96,17 @@ def tile_conv_1x1_9_layer_t_kernel(tc, x, weights, biases, grad_out, out):
             return w_full[i][:, :, cols(u)]
 
         def wide(i, r0, r1):
-            return w_full[i][:, r0:r1, STRIP:CIN].rearrange("p t (u c) -> p u t c", u=WIDE)
+            return w_full[i][:, r0:r1, WIDE0 * P : CIN].rearrange("p t (u c) -> p u t c", u=WIDE)
 
         def acc(u):
-            if u == 1:
-                return acc_one[:]
-            return acc_wide[:, u - STRIP_UNITS, :, :]
+            return acc_wide[:, u - WIDE0, :, :]
 
         sum_part = psum.tile([P, N_TILE], F32, name="bank")
         sum_all = psum.tile([P, N_TILE], F32, name="bank")
-        for target, unit, order in ((sum_part, 1, PE_PART), (sum_all, 0, tuple(range(LAYERS)))):
-            for i in order:
+        for i in range(LAYERS):
+            for target, unit, order in ((sum_all, 0, tuple(range(LAYERS))), (sum_part, 1, PE_PART)):
+                if i not in order:
+                    continue
                 nc.tensor.matmul(
                     out=target[:].rearrange("p (t c) -> p t c", t=PACK),
                     lhsT=ident[:],
@@ -171,7 +171,7 @@ def tile_conv_1x1_9_layer_t_kernel(tc, x, weights, biases, grad_out, out):
                         target = part[:]
                     else:
                         target = stg[:, h * N_TILE : (h + 1) * N_TILE]
-                    if u == LAST and h == 1:
+                    if u >= LAST - 1 and h == 1:
                         nc.vector.tensor_copy(out=target, in_=bank[:])
                     else:
                         nc.scalar.copy(out=target, in_=bank[:])
@@ -183,26 +183,22 @@ def tile_conv_1x1_9_layer_t_kernel(tc, x, weights, biases, grad_out, out):
         for r0, r1 in ROW_PIECES:
             nc.vector.tensor_tensor(out=acc_wide[:, :, r0:r1, :], in0=wide(0, r0, r1), in1=wide(1, r0, r1), op=ADD)
         for i in BASE_LAYERS:
-            if i == 3:
-                nc.vector.tensor_tensor(
-                    out=acc_one[:],
-                    in0=sum_part[:].rearrange("p (t c) -> p t c", t=PACK),
-                    in1=layer(3, 1),
-                    op=ADD,
-                )
-            if i == 4:
-                add_layer(1, 4)
             for r0, r1 in BASE_PIECES[i]:
                 nc.vector.tensor_tensor(out=acc_wide[:, :, r0:r1, :], in0=acc_wide[:, :, r0:r1, :], in1=wide(i, r0, r1), op=ADD)
         for n in range(4):
             quantise_g(n)
         quantise_w(0, 1)
         multiply(0)
-        for i in range(5, LAYERS):
-            add_layer(1, i)
+        add_layer(1, 5)
+        nc.vector.tensor_tensor(
+            out=acc(1),
+            in0=sum_part[:].rearrange("p (t c) -> p t c", t=PACK),
+            in1=acc(1),
+            op=ADD,
+        )
         nc.scalar.activation(
             out=w_grp[:, cols(1), :],
-            in_=acc_one[:].rearrange("p t c -> p c t"),
+            in_=acc(1).rearrange("p t c -> p c t"),
             func=COPY,
             scale=INV,
         )

@@ -27,8 +27,8 @@ INV = 1.0 / LAYERS
 FLOPS = 2 * BATCH * PIX * COUT * CIN
 BYTES = LAYERS * COUT * CIN * 2 + BATCH * COUT * PIX * 2 + BATCH * CIN * PIX * 4
 
-SPLIT_C = (6, 7, 8)
-STRIP_UNITS = 2
+SPLIT_C = (5, 6, 7, 8)
+STRIP_UNITS = 3
 STRIP = STRIP_UNITS * P
 WIDE0 = 1
 WIDE = UNITS - WIDE0
@@ -204,7 +204,7 @@ def tile_conv_1x1_9_layer_t_kernel(tc, x, weights, biases, grad_out, out):
         )
         quantise_w(1, 2)
         multiply(1)
-        for u in range(STRIP_UNITS, UNITS):
+        for u in range(2, UNITS):
             for i in range(5, LAYERS):
                 if u == LAST:
                     for r0 in (0, 2):

@@ -171,7 +171,7 @@ def tile_conv_1x1_9_layer_t_kernel(tc, x, weights, biases, grad_out, out):
                         target = part[:]
                     else:
                         target = stg[:, h * N_TILE : (h + 1) * N_TILE]
-                    if u >= LAST - 1 and h == 1:
+                    if u >= LAST and h == 1:
                         nc.vector.tensor_copy(out=target, in_=bank[:])
                     else:
                         nc.scalar.copy(out=target, in_=bank[:])
@@ -206,13 +206,7 @@ def tile_conv_1x1_9_layer_t_kernel(tc, x, weights, biases, grad_out, out):
         multiply(1)
         for u in range(2, UNITS):
             for i in range(5, LAYERS):
-                if u == LAST:
-                    for r0 in (0, 2):
-                        nc.vector.tensor_tensor(
-                            out=acc(u)[:, r0 : r0 + 2, :], in0=acc(u)[:, r0 : r0 + 2, :], in1=layer(i, u)[:, r0 : r0 + 2, :], op=ADD
-                        )
-                else:
-                    add_layer(u, i)
+                add_layer(u, i)
             nc.vector.tensor_scalar(
                 out=w_grp[:, cols(u), :],
                 in0=acc(u).rearrange("p t c -> p c t"),

@@ -178,7 +178,8 @@ def tile_conv_1x1_9_layer_t_kernel(tc, x, weights, biases, grad_out, out):
                     if fine:
                         nc.sync.dma_start(out=o_dram[b, u][:, h * N_TILE : (h + 1) * N_TILE], in_=target)
                 if not fine:
-                    nc.sync.dma_start(out=o_dram[b, u], in_=stg[:])
+                    queue = nc.scalar if b else nc.sync
+                    queue.dma_start(out=o_dram[b, u], in_=stg[:])
 
         for r0, r1 in ROW_PIECES:
             nc.vector.tensor_tensor(out=acc_wide[:, :, r0:r1, :], in0=wide(0, r0, r1), in1=wide(1, r0, r1), op=ADD)

from contextlib import ExitStack

import concourse.mybir as mybir
from concourse.masks import make_identity

F32 = mybir.dt.float32
BF16 = mybir.dt.bfloat16
U32 = mybir.dt.uint32
U8 = mybir.dt.uint8
E4M3X4 = mybir.dt.float8_e4m3fn_x4
E5M2X4 = mybir.dt.float8_e5m2_x4
ADD = mybir.AluOpType.add
MULT = mybir.AluOpType.mult
COPY = mybir.ActivationFunctionType.Copy

P = 128
PACK = 4
LAYERS = 9
COUT = 512
CIN = 1024
BATCH = 2
PIX = 1024
N_TILE = 512
UNITS = CIN // P
INV = 1.0 / LAYERS

FLOPS = 2 * BATCH * PIX * COUT * CIN
BYTES = LAYERS * COUT * CIN * 2 + BATCH * COUT * PIX * 2 + BATCH * CIN * PIX * 4

SPLIT_C = (5, 6, 7, 8)
STRIP_UNITS = 3
STRIP = STRIP_UNITS * P
WIDE0 = 1
WIDE = UNITS - WIDE0
ROW_PIECES = ((0, 1), (1, 2), (2, 3), (3, 4))
BASE_LAYERS = (2, 3, 4)
BASE_PIECES = {2: ((0, 2), (2, 4)), 3: ((0, 4),), 4: ((0, 4),)}
PE_PART = (6, 7, 8)
LAST = UNITS - 1


def tile_conv_1x1_9_layer_t_kernel(tc, x, weights, biases, grad_out, out):
    nc = tc.nc
    w_dram = weights.rearrange("i (p t) c a b -> i p t (c a b)", t=PACK)
    g_dram = grad_out.rearrange("b (p t) h v -> b p t (h v)", t=PACK)
    o_dram = out.rearrange("b (u m) h v -> b u m (h v)", m=P)

    with ExitStack() as ctx:
        keep = ctx.enter_context(tc.tile_pool(name="keep", bufs=1))
        stage = ctx.enter_context(tc.tile_pool(name="stage", bufs=8))
        psum = ctx.enter_context(tc.psum_pool(name="psum", bufs=8))

        ident = keep.tile([P, P], BF16, name="ident")
        make_identity(nc, ident[:])

        w_full = [keep.tile([P, PACK, CIN], BF16, name="w%d" % i) for i in range(SPLIT_C[0])]
        w_strip = {}
        w_rest = {}
        for i in SPLIT_C:
            w_strip[i] = keep.tile([P, PACK, STRIP], BF16, name="w%de" % i)
            w_rest[i] = keep.tile([P, PACK, CIN - STRIP], BF16, name="w%df" % i)
        g_raw = [keep.tile([P, PACK, PIX], BF16, name="g_raw%d" % b) for b in range(BATCH)]

        for r0, r1 in ROW_PIECES:
            for i in (0, 1):
                nc.sync.dma_start(out=w_full[i][:, r0:r1, :], in_=w_dram[i][:, r0:r1, :])
        for i in (2, 3):
            for r0, r1 in BASE_PIECES[i]:
                nc.sync.dma_start(out=w_full[i][:, r0:r1, :], in_=w_dram[i][:, r0:r1, :])
        nc.sync.dma_start(out=g_raw[0][:], in_=g_dram[0])
        nc.sync.dma_start(out=w_full[4][:], in_=w_dram[4])
        nc.sync.dma_start(out=g_raw[1][:], in_=g_dram[1])
        for i in range(5, SPLIT_C[0]):
            nc.sync.dma_start(out=w_full[i][:], in_=w_dram[i])
        for i in SPLIT_C:
            nc.sync.dma_start(out=w_strip[i][:], in_=w_dram[i][:, :, 0:STRIP])
        for i in SPLIT_C:
            nc.sync.dma_start(out=w_rest[i][:], in_=w_dram[i][:, :, STRIP:CIN])

        g_grp = [keep.tile([P, PIX, PACK], BF16, name="g_grp%d" % b, align_bytes=64) for b in range(BATCH)]
        g_codes = keep.tile([P, BATCH * PIX], U32, name="g_codes", align_bytes=64)
        g_scales = keep.tile([P, BATCH * PIX], U8, name="g_scales", align_bytes=64)
        w_grp = keep.tile([P, CIN, PACK], BF16, name="w_grp", align_bytes=64)
        w_codes = keep.tile([P, CIN], U32, name="w_codes", align_bytes=64)
        w_scales = keep.tile([P, CIN], U8, name="w_scales", align_bytes=64)
        acc_wide = keep.tile([P, WIDE, PACK, P], F32, name="acc_wide")

        def cols(u):
            return slice(u * P, (u + 1) * P)

        def layer(i, u):
            if i in SPLIT_C:
                if u < STRIP_UNITS:
                    return w_strip[i][:, :, cols(u)]
                return w_rest[i][:, :, cols(u - STRIP_UNITS)]
            return w_full[i][:, :, cols(u)]

        def wide(i, r0, r1):
            return w_full[i][:, r0:r1, WIDE0 * P : CIN].rearrange("p t (u c) -> p u t c", u=WIDE)

        def acc(u):
            return acc_wide[:, u - WIDE0, :, :]

        sum_part = psum.tile([P, N_TILE], F32, name="bank")
        sum_all = psum.tile([P, N_TILE], F32, name="bank")
        for i in range(LAYERS):
            for target, unit, order in ((sum_all, 0, tuple(range(LAYERS))), (sum_part, 1, PE_PART)):
                if i not in order:
                    continue
                nc.tensor.matmul(
                    out=target[:].rearrange("p (t c) -> p t c", t=PACK),
                    lhsT=ident[:],
                    rhs=layer(i, unit),
                    start=(i == order[0]),
                    stop=(i == order[-1]),
                )

        for n in range(4):
            b, h = divmod(n, 2)
            span = slice(h * N_TILE, (h + 1) * N_TILE)
            nc.scalar.copy(
                out=g_grp[b][:, span, :].rearrange("p (c i) t -> p c t i", i=4),
                in_=g_raw[b][:, :, span].rearrange("p t (c i) -> p c t i", i=4),
            )
        nc.scalar.activation(
            out=w_grp[:, cols(0), :],
            in_=sum_all[:].rearrange("p (t c) -> p c t", t=PACK),
            func=COPY,
            scale=INV,
        )

        def add_layer(u, i):
            nc.vector.tensor_tensor(out=acc(u), in0=acc(u), in1=layer(i, u), op=ADD)

        def quantise_g(n):
            b, h = divmod(n, 2)
            span = slice(h * N_TILE, (h + 1) * N_TILE)
            nc.vector.quantize_mx(
                out=g_codes[:, n * N_TILE : (n + 1) * N_TILE].bitcast(E5M2X4),
                scales=g_scales[:, n * N_TILE : (n + 1) * N_TILE],
                in_=g_grp[b][:, span, :].rearrange("p n t -> p (n t)"),
            )

        def quantise_w(u0, u1):
            span = slice(u0 * P, u1 * P)
            nc.vector.quantize_mx(
                out=w_codes[:, span].bitcast(E4M3X4),
                scales=w_scales[:, span],
                in_=w_grp[:, span, :].rearrange("p c t -> p (c t)"),
            )

        def multiply(u):
            fine = u in (LAST,)
            for b in range(BATCH):
                if not fine:
                    stg = stage.tile([P, PIX], F32, name="stg")
                for h in range(2):
                    n = 2 * b + h
                    bank = psum.tile([P, N_TILE], F32, name="bank")
                    nc.tensor.matmul_mx(
                        out=bank[:],
                        lhsT=w_codes[:, cols(u)].bitcast(E4M3X4),
                        lhsT_scale=w_scales[:, cols(u)],
                        rhs=g_codes[:, n * N_TILE : (n + 1) * N_TILE].bitcast(E5M2X4),
                        rhs_scale=g_scales[:, n * N_TILE : (n + 1) * N_TILE],
                        start=True,
                        stop=True,
                    )
                    if fine:
                        part = stage.tile([P, N_TILE], F32, name="part")
                        target = part[:]
                    else:
                        target = stg[:, h * N_TILE : (h + 1) * N_TILE]
                    if u >= LAST and h == 1:
                        nc.vector.tensor_copy(out=target, in_=bank[:])
                    else:
                        nc.scalar.copy(out=target, in_=bank[:])
                    if fine:
                        nc.sync.dma_start(out=o_dram[b, u][:, h * N_TILE : (h + 1) * N_TILE], in_=target)
                if not fine:
                    queue = nc.scalar if b else nc.sync
                    queue.dma_start(out=o_dram[b, u], in_=stg[:])

        for r0, r1 in ROW_PIECES:
            nc.vector.tensor_tensor(out=acc_wide[:, :, r0:r1, :], in0=wide(0, r0, r1), in1=wide(1, r0, r1), op=ADD)
        for i in BASE_LAYERS:
            for r0, r1 in BASE_PIECES[i]:
                nc.vector.tensor_tensor(out=acc_wide[:, :, r0:r1, :], in0=acc_wide[:, :, r0:r1, :], in1=wide(i, r0, r1), op=ADD)
        for n in range(4):
            quantise_g(n)
        quantise_w(0, 1)
        multiply(0)
        add_layer(1, 5)
        nc.vector.tensor_tensor(
            out=acc(1),
            in0=sum_part[:].rearrange("p (t c) -> p t c", t=PACK),
            in1=acc(1),
            op=ADD,
        )
        nc.scalar.activation(
            out=w_grp[:, cols(1), :],
            in_=acc(1).rearrange("p t c -> p c t"),
            func=COPY,
            scale=INV,
        )
        quantise_w(1, 2)
        multiply(1)
        for u in range(2, UNITS):
            for i in range(5, LAYERS):
                add_layer(u, i)
            nc.vector.tensor_scalar(
                out=w_grp[:, cols(u), :],
                in0=acc(u).rearrange("p t c -> p c t"),
                scalar1=INV,
                scalar2=None,
                op0=MULT,
            )
            quantise_w(u, u + 1)
            multiply(u)
